import numpy as np
import ml_dtypes


def mxq(x, axis, fmt="e4m3"):
    dtype, down = {"e4m3": (ml_dtypes.float8_e4m3fn, 7), "e5m2": (ml_dtypes.float8_e5m2, 14)}[fmt]
    v = np.moveaxis(np.asarray(x, np.float32).astype(ml_dtypes.bfloat16).astype(np.float64), axis, -1)
    blocks = v.reshape(v.shape[:-1] + (-1, 32))
    amax = np.abs(blocks).max(-1, keepdims=True)
    byte = np.maximum(np.where(amax > 0, np.frexp(amax)[1] - 1 + 127, 0) - down, 1)
    scale = np.exp2(byte - 127.0)
    codes = (blocks / scale).astype(np.float32).astype(dtype).astype(np.float64)
    return np.moveaxis((codes * scale).reshape(v.shape), -1, axis)


WIDE = False


def mx_kscale(k):
    if not WIDE:
        return np.ones(k)
    levels = np.array([10, -10, 5, -5, 0])
    if k % 512:
        return np.exp2(np.random.permutation(np.resize(levels, k // 32))).repeat(32)
    a = np.empty((k // 512, 16))
    for p in range(k // 512):
        a[p, :8] = np.random.permutation(np.resize(levels, 8))
        for g in range(8):
            far = levels[np.abs(levels - a[p, g]) >= 10]
            a[p, g + 8] = far[np.random.randint(len(far))]
    return np.exp2(a.ravel()).repeat(32)


BF16 = ml_dtypes.bfloat16


def bf(x):
    return np.asarray(x, np.float32).astype(BF16)


def f64(x):
    return np.asarray(x).astype(np.float64)


B, S, U, G, G2, N = 640, 10, 40, 512, 1024, 128


def setup_inputs():
    s, t = mx_kscale(G), mx_kscale(G2)
    e = np.exp(np.random.standard_normal((B, S)))
    return {"g1": bf(np.maximum(np.random.standard_normal((B, S, G)), 0.0) * s),
            "iab": bf(e / e.sum(1, keepdims=True)),
            "sW2": bf(np.random.standard_normal((G2, G)) * np.sqrt(2.0 / G) / s * t[:, None]),
            "sb2": bf(np.random.standard_normal(G2) * 0.3 * t),
            "sW3": bf(np.random.standard_normal((N, G2)) * 1.5 * np.sqrt(2.0 / G2) / t),
            "sb3": bf(np.random.standard_normal(N) * 0.5)}


def reference(g1, iab, sW2, sb2, sW3, sb3):
    h = np.maximum((mxq(f64(g1), 2, "e4m3") @ mxq(f64(sW2), 1, "e4m3").T) + f64(sb2), 0.0)
    z = (mxq(h, 2, "e4m3") @ mxq(f64(sW3), 1, "e4m3").T) + f64(sb3)
    e = np.exp(z - z.max(-1, keepdims=True))
    return e / e.sum(-1, keepdims=True) * f64(iab)[:, :, None]

@@ -1,0 +1,344 @@
+from contextlib import ExitStack
+
+import concourse.mybir as mybir
+from concourse.masks import make_identity
+
+F32 = mybir.dt.float32
+BF16 = mybir.dt.bfloat16
+U32 = mybir.dt.uint32
+U8 = mybir.dt.uint8
+FP8X4 = mybir.dt.float8_e4m3fn_x4
+ACT = mybir.ActivationFunctionType
+ALU = mybir.AluOpType
+AX = mybir.AxisListType
+
+P = 128
+TOKENS = 6400
+G = 512
+G2 = 1024
+NOUT = 128
+SUBS = TOKENS // P
+FLOPS = 2 * TOKENS * G * G2 + 2 * TOKENS * G2 * NOUT
+
+PINNED = False
+LOOK = 3
+LAG = 2
+
+
+def tile_resourceallocationnetwork_pa_t_kernel(tc, g1, iab, sW2, sb2, sW3, sb3, out):
+    nc = tc.nc
+    nsubs = [4] * (SUBS // 4) + ([SUBS % 4] if SUBS % 4 else [])
+    ns = len(nsubs)
+
+    g1v = g1.flatten_outer_dims().rearrange("(p i) k -> p (i k)", i=SUBS)
+    outv = out.flatten_outer_dims().rearrange("(p i) n -> p i n", i=SUBS)
+    iabv = iab.rearrange("(p q) s -> p (q s)", p=P)
+    w2v = sW2.rearrange("(g p t) k -> g p (t k)", g=2, t=4)
+    b2v = sb2.rearrange("(g p t) -> p g t", g=2, t=4)
+
+    with ExitStack() as ctx:
+        if PINNED:
+            ctx.enter_context(tc.manual_schedule())
+        const = ctx.enter_context(tc.tile_pool(name="const", bufs=1))
+        raw = ctx.enter_context(tc.tile_pool(name="raw", bufs=1))
+        keep = ctx.enter_context(tc.tile_pool(name="keep", bufs=1))
+        xgp = ctx.enter_context(tc.tile_pool(name="xgp", bufs=5))
+        hpp = ctx.enter_context(tc.tile_pool(name="hpp", bufs=4))
+        hgp = ctx.enter_context(tc.tile_pool(name="hgp", bufs=3))
+        hcp = ctx.enter_context(tc.tile_pool(name="hcp", bufs=6))
+        epp = ctx.enter_context(tc.tile_pool(name="epp", bufs=3))
+        sml = ctx.enter_context(tc.tile_pool(name="sml", bufs=4))
+        psum = ctx.enter_context(tc.psum_pool(name="psum", bufs=1))
+
+        ident = const.tile([P, P], F32, name="ident")
+        make_identity(nc, ident[:])
+        warm_in = const.tile([P, 1], F32, name="warm_in")
+        warm_out = const.tile([P, 1], F32, name="warm_out")
+        nc.vector.memset(warm_in[:], 0.0)
+        nc.scalar.activation(out=warm_out[:], in_=warm_in[:], func=ACT.Exp)
+
+        b2raw = const.tile([P, 2, 4], BF16, name="b2raw")
+        c3raw = const.tile([P, NOUT], BF16, name="c3raw")
+        iabraw = const.tile([P, SUBS], BF16, name="iabraw")
+        nc.scalar.dma_start(out=b2raw[:], in_=b2v)
+        nc.scalar.dma_start(out=c3raw[:], in_=sb3.partition_broadcast(P))
+        nc.scalar.dma_start(out=iabraw[:], in_=iabv)
+
+        w2raw = [raw.tile([P, 4 * G], BF16, name="w2raw%d" % g) for g in range(2)]
+        w3raw = raw.tile([P, G2], BF16, name="w3raw")
+        g1t = [raw.tile([P, nsubs[s] * G], BF16, name="g1t%d" % s) for s in range(ns)]
+
+        def load_g1(s):
+            nc.sync.dma_start(out=g1t[s][:], in_=g1v[:, 4 * G * s : 4 * G * s + nsubs[s] * G])
+
+        nc.sync.dma_start(out=w2raw[0][:], in_=w2v[0])
+        load_g1(0)
+        nc.sync.dma_start(out=w2raw[1][:], in_=w2v[1])
+        load_g1(1)
+        nc.sync.dma_start(out=w3raw[:], in_=sW3)
+        for s in range(2, ns):
+            load_g1(s)
+
+        w2c = [keep.tile([P, 512], U32, name="w2c%d" % g, align_bytes=64) for g in range(2)]
+        w2s = [keep.tile([P, 512], U8, name="w2s%d" % g, align_bytes=64) for g in range(2)]
+        w3c = keep.tile([P, 256], U32, name="w3c", align_bytes=64)
+        w3s = keep.tile([P, 256], U8, name="w3s", align_bytes=64)
+        xc = [keep.tile([P, P * nsubs[s]], U32, name="xc%d" % s, align_bytes=64) for s in range(ns)]
+        xs = [keep.tile([P, P * nsubs[s]], U8, name="xs%d" % s, align_bytes=64) for s in range(ns)]
+        b2f = const.tile([P, 8], F32, name="b2f")
+        c3f = const.tile([P, NOUT], F32, name="c3f")
+        iabf = const.tile([P, SUBS], F32, name="iabf")
+
+        banks = {}
+        grouped = {}
+
+        def words_step2(tile_ap):
+            w32 = tile_ap.bitcast(F32)
+            return lambda j, u: w32[:, 256 * j + u : 256 * j + 256 : 2]
+
+        def xt(key, words, nsub, bank_ids):
+            for b in range(nsub // 2):
+                xp = psum.tile([P, 2, 256], F32, name="xp", tag="bank%d" % bank_ids[b])
+                for jj in range(2):
+                    for u in range(2):
+                        nc.tensor.transpose(xp[:, u, P * jj : P * jj + P], words(2 * b + jj, u), ident[:])
+                banks[(key, b)] = xp
+
+        def xe(key, b, on_scalar):
+            if b == 0:
+                grouped[key] = xgp.tile([P, 4 * P * 2], F32, name="xg", align_bytes=64)
+            dst = grouped[key][:, 512 * b : 512 * b + 512].rearrange("p (w u) -> p w u", u=2)
+            src = banks[(key, b)][:].rearrange("p u w -> p w u")
+            if on_scalar:
+                nc.scalar.copy(out=dst, in_=src)
+            else:
+                nc.vector.tensor_copy(out=dst, in_=src)
+
+        def xq(key, nsub, codes, scales):
+            nc.vector.quantize_mx(
+                out=codes.bitcast(FP8X4), scales=scales, in_=grouped[key][:, : 2 * P * nsub].bitcast(BF16)
+            )
+
+        def x_t(s, bank_ids):
+            if 0 <= s < ns:
+                xt(s, words_step2(g1t[s][:]), nsubs[s], bank_ids)
+
+        def x_e(s, second_on_scalar):
+            if 0 <= s < ns:
+                xe(s, 0, True)
+                if nsubs[s] == 4:
+                    xe(s, 1, second_on_scalar)
+
+        def x_q(s):
+            if 0 <= s < ns:
+                xq(s, nsubs[s], xc[s][:], xs[s][:])
+
+        hb = {}
+        hp = {}
+        hg = {}
+        hc = {}
+        hs = {}
+        zb = {}
+        nzc = {}
+        mn = {}
+        ex = {}
+        ss = {}
+        rs = {}
+
+        def l1(s, g, t):
+            if not 0 <= s < ns:
+                return
+            w = P * nsubs[s]
+            hb_t = psum.tile([P, w], F32, name="hb", tag="bank%d" % (4 + t))
+            nc.tensor.matmul_mx(
+                out=hb_t[:],
+                lhsT=w2c[g][:, P * t : P * t + P].bitcast(FP8X4),
+                lhsT_scale=w2s[g][:, P * t : P * t + P],
+                rhs=xc[s][:].bitcast(FP8X4),
+                rhs_scale=xs[s][:],
+                start=True,
+                stop=True,
+            )
+            hb[(s, g, t)] = hb_t
+
+        def ev(s, g, t):
+            if not 0 <= s < ns:
+                return
+            w = P * nsubs[s]
+            if t == 0:
+                hp[(s, g)] = hpp.tile([P, 4, w], BF16, name="hp")
+            nc.scalar.activation(
+                out=hp[(s, g)][:, t, :],
+                in_=hb[(s, g, t)][:],
+                func=ACT.Relu,
+                bias=b2f[:, 4 * g + t : 4 * g + t + 1],
+                scale=1.0,
+            )
+
+        def rg(s, g):
+            if not 0 <= s < ns:
+                return
+            w = P * nsubs[s]
+            hg_t = hgp.tile([P, 4 * w], BF16, name="hg", align_bytes=64)
+            nc.vector.tensor_copy(
+                out=hg_t[:].rearrange("p (c i t) -> p c t i", i=4, t=4),
+                in_=hp[(s, g)][:].rearrange("p t (c i) -> p c t i", i=4),
+            )
+            hg[(s, g)] = hg_t
+
+        def hq(s, g):
+            if not 0 <= s < ns:
+                return
+            w = P * nsubs[s]
+            hc_t = hcp.tile([P, w], U32, name="hc", align_bytes=64)
+            hs_t = hcp.tile([P, w], U8, name="hs", align_bytes=64)
+            nc.vector.quantize_mx(out=hc_t[:].bitcast(FP8X4), scales=hs_t[:], in_=hg[(s, g)][:])
+            hc[(s, g)] = hc_t
+            hs[(s, g)] = hs_t
+
+        def l2(s):
+            if not 0 <= s < ns:
+                return
+            zb_t = psum.tile([P, 4, NOUT], F32, name="zb", tag="bank%d" % (2 + s % 2))
+            for j in range(nsubs[s]):
+                for g in range(2):
+                    nc.tensor.matmul_mx(
+                        out=zb_t[:, j, :],
+                        lhsT=hc[(s, g)][:, P * j : P * j + P].bitcast(FP8X4),
+                        lhsT_scale=hs[(s, g)][:, P * j : P * j + P],
+                        rhs=w3c[:, P * g : P * g + P].bitcast(FP8X4),
+                        rhs_scale=w3s[:, P * g : P * g + P],
+                        start=(g == 0),
+                        stop=(g == 1),
+                    )
+            zb[s] = zb_t
+
+        def stt(s):
+            if not 0 <= s < ns:
+                return
+            n = nsubs[s]
+            nzc_t = epp.tile([P, 4, NOUT], F32, name="nzc")
+            nc.vector.scalar_tensor_tensor(
+                out=nzc_t[:, :n, :],
+                in0=zb[s][:, :n, :],
+                scalar=-1.0,
+                in1=c3f[:].unsqueeze(1).to_broadcast([P, n, NOUT]),
+                op0=ALU.mult,
+                op1=ALU.subtract,
+            )
+            nzc[s] = nzc_t
+
+        def mnr(s):
+            if not 0 <= s < ns:
+                return
+            n = nsubs[s]
+            mn_t = sml.tile([P, 4], F32, name="mn")
+            nc.vector.tensor_reduce(out=mn_t[:, :n], in_=nzc[s][:, :n, :], axis=AX.X, op=ALU.min)
+            mn[s] = mn_t
+
+        def ep2(s):
+            if not 0 <= s < ns:
+                return
+            ex_t = epp.tile([P, 4, NOUT], F32, name="ex")
+            ss_t = sml.tile([P, 4], F32, name="ss")
+            for j in range(nsubs[s]):
+                nc.scalar.activation(
+                    out=ex_t[:, j, :],
+                    in_=nzc[s][:, j, :],
+                    func=ACT.Exp,
+                    bias=mn[s][:, j : j + 1],
+                    scale=-1.0,
+                    accum_out=ss_t[:, j : j + 1],
+                )
+            ex[s] = ex_t
+            ss[s] = ss_t
+
+        def rc(s):
+            if not 0 <= s < ns:
+                return
+            n = nsubs[s]
+            rs_t = sml.tile([P, 4], F32, name="rs")
+            nc.vector.reciprocal(out=rs_t[:, :n], in_=ss[s][:, :n])
+            rs[s] = rs_t
+
+        def ts(s):
+            if not 0 <= s < ns:
+                return
+            n = nsubs[s]
+            ot = epp.tile([P, 4, NOUT], F32, name="ot")
+            for j in range(n):
+                nc.vector.tensor_scalar(
+                    out=ot[:, j, :],
+                    in0=ex[s][:, j, :],
+                    scalar1=rs[s][:, j : j + 1],
+                    scalar2=iabf[:, 4 * s + j : 4 * s + j + 1],
+                    op0=ALU.mult,
+                    op1=ALU.mult,
+                )
+            nc.sync.dma_start(out=outv[:, 4 * s : 4 * s + n, :], in_=ot[:, :n, :])
+
+        xt("w20", words_step2(w2raw[0][:]), 4, [4, 5])
+        x_t(0, [6, 7])
+        xt("w21", words_step2(w2raw[1][:]), 4, [0, 1])
+        x_t(1, [2, 3])
+        xe("w20", 0, True)
+        xe("w20", 1, False)
+        xe(0, 0, True)
+        xe(0, 1, False)
+        xq("w20", 4, w2c[0][:], w2s[0][:])
+        xe("w21", 0, True)
+        xe("w21", 1, False)
+        x_q(0)
+        nc.vector.tensor_copy(out=b2f[:], in_=b2raw[:].rearrange("p g t -> p (g t)"))
+        for t in range(4):
+            l1(0, 0, t)
+        xt("w3", words_step2(w3raw[:]), 2, [0])
+        xe(1, 0, True)
+        xe(1, 1, False)
+        xq("w21", 4, w2c[1][:], w2s[1][:])
+        x_t(2, [1, 2])
+        xe("w3", 0, False)
+        x_q(1)
+        xe(2, 0, False)
+        xq("w3", 2, w3c[:], w3s[:])
+        xe(2, 1, False)
+        x_t(3, [3, 0])
+        nc.vector.tensor_copy(out=c3f[:], in_=c3raw[:])
+        nc.vector.tensor_copy(out=iabf[:], in_=iabraw[:])
+
+        for s in range(ns):
+            rg(s - 1, 1)
+            rc(s - 3)
+            stt(s - 2)
+            hq(s - 1, 1)
+            ts(s - 3)
+            mnr(s - 2)
+            for t in range(4):
+                ev(s, 0, t)
+                l1(s, 1, t)
+            l2(s - 1)
+            x_e(s + LOOK, (s + LOOK) % 3 == 0)
+            rg(s, 0)
+            x_q(s + LOOK - 1)
+            hq(s, 0)
+            for t in range(4):
+                ev(s, 1, t)
+                l1(s + 1, 0, t)
+            x_t(s + LOOK + 1, [0, 1])
+            ep2(s - 2)
+
+        rg(ns - 1, 1)
+        stt(ns - 2)
+        hq(ns - 1, 1)
+        mnr(ns - 2)
+        l2(ns - 1)
+        rc(ns - 3)
+        ep2(ns - 2)
+        ts(ns - 3)
+        stt(ns - 1)
+        rc(ns - 2)
+        mnr(ns - 1)
+        ts(ns - 2)
+        ep2(ns - 1)
+        rc(ns - 1)
+        ts(ns - 1)

@@ -267,7 +267,7 @@ def tile_resourceallocationnetwork_pa_t_kernel(tc, g1, iab, sW2, sb2, sW3, sb3, 
             n = nsubs[s]
             ot = epp.tile([P, 4, NOUT], F32, name="ot")
             for j in range(n):
-                nc.vector.tensor_scalar(
+                nc.gpsimd.tensor_scalar(
                     out=ot[:, j, :],
                     in0=ex[s][:, j, :],
                     scalar1=rs[s][:, j : j + 1],

@@ -267,7 +267,7 @@ def tile_resourceallocationnetwork_pa_t_kernel(tc, g1, iab, sW2, sb2, sW3, sb3, 
             n = nsubs[s]
             ot = epp.tile([P, 4, NOUT], F32, name="ot")
             for j in range(n):
-                nc.gpsimd.tensor_scalar(
+                (nc.gpsimd if s < ns - 3 else nc.vector).tensor_scalar(
                     out=ot[:, j, :],
                     in0=ex[s][:, j, :],
                     scalar1=rs[s][:, j : j + 1],
@@ -317,7 +317,7 @@ def tile_resourceallocationnetwork_pa_t_kernel(tc, g1, iab, sW2, sb2, sW3, sb3, 
                 ev(s, 0, t)
                 l1(s, 1, t)
             l2(s - 1)
-            x_e(s + LOOK, (s + LOOK) % 3 == 0)
+            x_e(s + LOOK, False)
             rg(s, 0)
             x_q(s + LOOK - 1)
             hq(s, 0)

@@ -21,14 +21,15 @@ SUBS = TOKENS // P
 FLOPS = 2 * TOKENS * G * G2 + 2 * TOKENS * G2 * NOUT
 
 PINNED = False
-LOOK = 3
+LOOK = 2
 LAG = 2
 
 
 def tile_resourceallocationnetwork_pa_t_kernel(tc, g1, iab, sW2, sb2, sW3, sb3, out):
     nc = tc.nc
-    nsubs = [4] * (SUBS // 4) + ([SUBS % 4] if SUBS % 4 else [])
+    nsubs = [2] + [4] * 11 + [2, 2]
     ns = len(nsubs)
+    first = [sum(nsubs[:s]) for s in range(ns)]
 
     g1v = g1.flatten_outer_dims().rearrange("(p i) k -> p (i k)", i=SUBS)
     outv = out.flatten_outer_dims().rearrange("(p i) n -> p i n", i=SUBS)
@@ -61,22 +62,30 @@ def tile_resourceallocationnetwork_pa_t_kernel(tc, g1, iab, sW2, sb2, sW3, sb3, 
         c3raw = const.tile([P, NOUT], BF16, name="c3raw")
         iabraw = const.tile([P, SUBS], BF16, name="iabraw")
         nc.scalar.dma_start(out=b2raw[:], in_=b2v)
-        nc.scalar.dma_start(out=c3raw[:], in_=sb3.partition_broadcast(P))
-        nc.scalar.dma_start(out=iabraw[:], in_=iabv)
 
         w2raw = [raw.tile([P, 4 * G], BF16, name="w2raw%d" % g) for g in range(2)]
         w3raw = raw.tile([P, G2], BF16, name="w3raw")
         g1t = [raw.tile([P, nsubs[s] * G], BF16, name="g1t%d" % s) for s in range(ns)]
 
         def load_g1(s):
-            nc.sync.dma_start(out=g1t[s][:], in_=g1v[:, 4 * G * s : 4 * G * s + nsubs[s] * G])
+            nc.sync.dma_start(out=g1t[s][:], in_=g1v[:, G * first[s] : G * (first[s] + nsubs[s])])
 
-        nc.sync.dma_start(out=w2raw[0][:], in_=w2v[0])
+        def load_w2(g, b):
+            cols = slice(2 * G * b, 2 * G * b + 2 * G)
+            nc.sync.dma_start(out=w2raw[g][:, cols], in_=w2v[g][:, cols])
+
+        load_w2(0, 0)
         load_g1(0)
-        nc.sync.dma_start(out=w2raw[1][:], in_=w2v[1])
+        load_w2(0, 1)
+        load_w2(1, 0)
+        load_w2(1, 1)
         load_g1(1)
         nc.sync.dma_start(out=w3raw[:], in_=sW3)
-        for s in range(2, ns):
+        for s in range(2, 5):
+            load_g1(s)
+        nc.sync.dma_start(out=c3raw[:], in_=sb3.partition_broadcast(P))
+        nc.sync.dma_start(out=iabraw[:], in_=iabv)
+        for s in range(5, ns):
             load_g1(s)
 
         w2c = [keep.tile([P, 512], U32, name="w2c%d" % g, align_bytes=64) for g in range(2)]
@@ -96,9 +105,9 @@ def tile_resourceallocationnetwork_pa_t_kernel(tc, g1, iab, sW2, sb2, sW3, sb3, 
             w32 = tile_ap.bitcast(F32)
             return lambda j, u: w32[:, 256 * j + u : 256 * j + 256 : 2]
 
-        def xt(key, words, nsub, bank_ids):
-            for b in range(nsub // 2):
-                xp = psum.tile([P, 2, 256], F32, name="xp", tag="bank%d" % bank_ids[b])
+        def xt(key, words, blocks, bank_ids):
+            for b in blocks:
+                xp = psum.tile([P, 2, 256], F32, name="xp", tag="bank%d" % bank_ids[b - blocks[0]])
                 for jj in range(2):
                     for u in range(2):
                         nc.tensor.transpose(xp[:, u, P * jj : P * jj + P], words(2 * b + jj, u), ident[:])
@@ -114,14 +123,23 @@ def tile_resourceallocationnetwork_pa_t_kernel(tc, g1, iab, sW2, sb2, sW3, sb3, 
             else:
                 nc.vector.tensor_copy(out=dst, in_=src)
 
-        def xq(key, nsub, codes, scales):
+        def xq(key, nsub, codes, scales, b=0):
             nc.vector.quantize_mx(
-                out=codes.bitcast(FP8X4), scales=scales, in_=grouped[key][:, : 2 * P * nsub].bitcast(BF16)
+                out=codes.bitcast(FP8X4),
+                scales=scales,
+                in_=grouped[key][:, 512 * b : 512 * b + 2 * P * nsub].bitcast(BF16),
             )
+
+        def w2_t(g, b, bank):
+            xt("w2%d" % g, words_step2(w2raw[g][:]), [b], [bank])
+
+        def w2_q(g, b):
+            cols = slice(256 * b, 256 * b + 256)
+            xq("w2%d" % g, 2, w2c[g][:, cols], w2s[g][:, cols], b)
 
         def x_t(s, bank_ids):
             if 0 <= s < ns:
-                xt(s, words_step2(g1t[s][:]), nsubs[s], bank_ids)
+                xt(s, words_step2(g1t[s][:]), list(range(nsubs[s] // 2)), bank_ids)
 
         def x_e(s, second_on_scalar):
             if 0 <= s < ns:
@@ -271,40 +289,36 @@ def tile_resourceallocationnetwork_pa_t_kernel(tc, g1, iab, sW2, sb2, sW3, sb3, 
                     out=ot[:, j, :],
                     in0=ex[s][:, j, :],
                     scalar1=rs[s][:, j : j + 1],
-                    scalar2=iabf[:, 4 * s + j : 4 * s + j + 1],
+                    scalar2=iabf[:, first[s] + j : first[s] + j + 1],
                     op0=ALU.mult,
                     op1=ALU.mult,
                 )
-            nc.sync.dma_start(out=outv[:, 4 * s : 4 * s + n, :], in_=ot[:, :n, :])
+            nc.sync.dma_start(out=outv[:, first[s] : first[s] + n, :], in_=ot[:, :n, :])
 
-        xt("w20", words_step2(w2raw[0][:]), 4, [4, 5])
-        x_t(0, [6, 7])
-        xt("w21", words_step2(w2raw[1][:]), 4, [0, 1])
-        x_t(1, [2, 3])
+        w2_t(0, 0, 0)
+        x_t(0, [1])
+        w2_t(0, 1, 2)
+        w2_t(1, 0, 3)
         xe("w20", 0, True)
-        xe("w20", 1, False)
-        xe(0, 0, True)
-        xe(0, 1, False)
-        xq("w20", 4, w2c[0][:], w2s[0][:])
-        xe("w21", 0, True)
-        xe("w21", 1, False)
+        xe(0, 0, False)
+        xe("w20", 1, True)
+        w2_q(0, 0)
         x_q(0)
-        nc.vector.tensor_copy(out=b2f[:], in_=b2raw[:].rearrange("p g t -> p (g t)"))
+        w2_q(0, 1)
+        nc.gpsimd.tensor_copy(out=b2f[:], in_=b2raw[:].rearrange("p g t -> p (g t)"))
         for t in range(4):
             l1(0, 0, t)
-        xt("w3", words_step2(w3raw[:]), 2, [0])
-        xe(1, 0, True)
+        xe("w21", 0, True)
+        w2_t(1, 1, 0)
+        xe("w21", 1, True)
+        x_t(1, [1, 2])
+        xe(1, 0, False)
+        w2_q(1, 0)
+        w2_q(1, 1)
         xe(1, 1, False)
-        xq("w21", 4, w2c[1][:], w2s[1][:])
-        x_t(2, [1, 2])
-        xe("w3", 0, False)
         x_q(1)
-        xe(2, 0, False)
-        xq("w3", 2, w3c[:], w3s[:])
-        xe(2, 1, False)
-        x_t(3, [3, 0])
-        nc.vector.tensor_copy(out=c3f[:], in_=c3raw[:])
-        nc.vector.tensor_copy(out=iabf[:], in_=iabraw[:])
+        nc.gpsimd.tensor_copy(out=c3f[:], in_=c3raw[:])
+        nc.gpsimd.tensor_copy(out=iabf[:], in_=iabraw[:])
 
         for s in range(ns):
             rg(s - 1, 1)
@@ -312,14 +326,21 @@ def tile_resourceallocationnetwork_pa_t_kernel(tc, g1, iab, sW2, sb2, sW3, sb3, 
             stt(s - 2)
             hq(s - 1, 1)
             ts(s - 3)
+            if s > 0:
+                x_q(s + 1)
             mnr(s - 2)
             for t in range(4):
                 ev(s, 0, t)
                 l1(s, 1, t)
             l2(s - 1)
-            x_e(s + LOOK, False)
+            if s == 0:
+                x_t(2, [0, 1])
+                xt("w3", words_step2(w3raw[:]), [0], [3])
+                xe("w3", 0, False)
             rg(s, 0)
-            x_q(s + LOOK - 1)
+            x_e(s + LOOK, False)
+            if s == 0:
+                xq("w3", 2, w3c[:], w3s[:])
             hq(s, 0)
             for t in range(4):
                 ev(s, 1, t)

@@ -20,7 +20,6 @@ NOUT = 128
 SUBS = TOKENS // P
 FLOPS = 2 * TOKENS * G * G2 + 2 * TOKENS * G2 * NOUT
 
-PINNED = False
 LOOK = 2
 LAG = 2
 
@@ -38,17 +37,15 @@ def tile_resourceallocationnetwork_pa_t_kernel(tc, g1, iab, sW2, sb2, sW3, sb3, 
     b2v = sb2.rearrange("(g p t) -> p g t", g=2, t=4)
 
     with ExitStack() as ctx:
-        if PINNED:
-            ctx.enter_context(tc.manual_schedule())
         const = ctx.enter_context(tc.tile_pool(name="const", bufs=1))
         raw = ctx.enter_context(tc.tile_pool(name="raw", bufs=1))
         keep = ctx.enter_context(tc.tile_pool(name="keep", bufs=1))
         xgp = ctx.enter_context(tc.tile_pool(name="xgp", bufs=5))
-        hpp = ctx.enter_context(tc.tile_pool(name="hpp", bufs=4))
+        hpp = ctx.enter_context(tc.tile_pool(name="hpp", bufs=6))
         hgp = ctx.enter_context(tc.tile_pool(name="hgp", bufs=3))
         hcp = ctx.enter_context(tc.tile_pool(name="hcp", bufs=6))
-        epp = ctx.enter_context(tc.tile_pool(name="epp", bufs=3))
-        sml = ctx.enter_context(tc.tile_pool(name="sml", bufs=4))
+        epp = ctx.enter_context(tc.tile_pool(name="epp", bufs=4))
+        sml = ctx.enter_context(tc.tile_pool(name="sml", bufs=6))
         psum = ctx.enter_context(tc.psum_pool(name="psum", bufs=1))
 
         ident = const.tile([P, P], F32, name="ident")
@@ -285,7 +282,7 @@ def tile_resourceallocationnetwork_pa_t_kernel(tc, g1, iab, sW2, sb2, sW3, sb3, 
             n = nsubs[s]
             ot = epp.tile([P, 4, NOUT], F32, name="ot")
             for j in range(n):
-                (nc.gpsimd if s < ns - 3 else nc.vector).tensor_scalar(
+                (nc.gpsimd if s < ns - 4 else nc.vector).tensor_scalar(
                     out=ot[:, j, :],
                     in0=ex[s][:, j, :],
                     scalar1=rs[s][:, j : j + 1],
@@ -321,14 +318,15 @@ def tile_resourceallocationnetwork_pa_t_kernel(tc, g1, iab, sW2, sb2, sW3, sb3, 
         nc.gpsimd.tensor_copy(out=iabf[:], in_=iabraw[:])
 
         for s in range(ns):
-            rg(s - 1, 1)
-            rc(s - 3)
-            stt(s - 2)
-            hq(s - 1, 1)
-            ts(s - 3)
             if s > 0:
                 x_q(s + 1)
+            rg(s - 1, 1)
+            rc(s - 4)
+            stt(s - 2)
+            hq(s - 1, 1)
+            ts(s - 4)
             mnr(s - 2)
+            ep2(s - 3)
             for t in range(4):
                 ev(s, 0, t)
                 l1(s, 1, t)
@@ -346,13 +344,15 @@ def tile_resourceallocationnetwork_pa_t_kernel(tc, g1, iab, sW2, sb2, sW3, sb3, 
                 ev(s, 1, t)
                 l1(s + 1, 0, t)
             x_t(s + LOOK + 1, [0, 1])
-            ep2(s - 2)
 
-        rg(ns - 1, 1)
+        ep2(ns - 3)
         stt(ns - 2)
-        hq(ns - 1, 1)
+        rc(ns - 4)
+        rg(ns - 1, 1)
         mnr(ns - 2)
+        hq(ns - 1, 1)
         l2(ns - 1)
+        ts(ns - 4)
         rc(ns - 3)
         ep2(ns - 2)
         ts(ns - 3)

@@ -45,6 +45,7 @@ def tile_resourceallocationnetwork_pa_t_kernel(tc, g1, iab, sW2, sb2, sW3, sb3, 
         hgp = ctx.enter_context(tc.tile_pool(name="hgp", bufs=3))
         hcp = ctx.enter_context(tc.tile_pool(name="hcp", bufs=6))
         epp = ctx.enter_context(tc.tile_pool(name="epp", bufs=4))
+        otp = ctx.enter_context(tc.tile_pool(name="otp", bufs=6))
         sml = ctx.enter_context(tc.tile_pool(name="sml", bufs=6))
         psum = ctx.enter_context(tc.psum_pool(name="psum", bufs=1))
 
@@ -164,7 +165,7 @@ def tile_resourceallocationnetwork_pa_t_kernel(tc, g1, iab, sW2, sb2, sW3, sb3, 
             if not 0 <= s < ns:
                 return
             w = P * nsubs[s]
-            hb_t = psum.tile([P, w], F32, name="hb", tag="bank%d" % (4 + t))
+            hb_t = psum.tile([P, w], F32, name="hb", tag="bank%d" % (3 + ((2 * s + g) * 4 + t) % 5))
             nc.tensor.matmul_mx(
                 out=hb_t[:],
                 lhsT=w2c[g][:, P * t : P * t + P].bitcast(FP8X4),
@@ -214,7 +215,7 @@ def tile_resourceallocationnetwork_pa_t_kernel(tc, g1, iab, sW2, sb2, sW3, sb3, 
         def l2(s):
             if not 0 <= s < ns:
                 return
-            zb_t = psum.tile([P, 4, NOUT], F32, name="zb", tag="bank%d" % (2 + s % 2))
+            zb_t = psum.tile([P, 4, NOUT], F32, name="zb", tag="bank2")
             for j in range(nsubs[s]):
                 for g in range(2):
                     nc.tensor.matmul_mx(
@@ -280,7 +281,7 @@ def tile_resourceallocationnetwork_pa_t_kernel(tc, g1, iab, sW2, sb2, sW3, sb3, 
             if not 0 <= s < ns:
                 return
             n = nsubs[s]
-            ot = epp.tile([P, 4, NOUT], F32, name="ot")
+            ot = otp.tile([P, 4, NOUT], F32, name="ot")
             for j in range(n):
                 (nc.gpsimd if s < ns - 4 else nc.vector).tensor_scalar(
                     out=ot[:, j, :],
@@ -295,7 +296,7 @@ def tile_resourceallocationnetwork_pa_t_kernel(tc, g1, iab, sW2, sb2, sW3, sb3, 
         w2_t(0, 0, 0)
         x_t(0, [1])
         w2_t(0, 1, 2)
-        w2_t(1, 0, 3)
+        w2_t(1, 0, 7)
         xe("w20", 0, True)
         xe(0, 0, False)
         xe("w20", 1, True)
@@ -312,11 +313,12 @@ def tile_resourceallocationnetwork_pa_t_kernel(tc, g1, iab, sW2, sb2, sW3, sb3, 
         xe(1, 0, False)
         w2_q(1, 0)
         w2_q(1, 1)
-        xe(1, 1, False)
+        xe(1, 1, True)
         x_q(1)
         nc.gpsimd.tensor_copy(out=c3f[:], in_=c3raw[:])
         nc.gpsimd.tensor_copy(out=iabf[:], in_=iabraw[:])
 
+        ctx.enter_context(tc.manual_schedule(engines={mybir.EngineType.PE}))
         for s in range(ns):
             if s > 0:
                 x_q(s + 1)
@@ -333,7 +335,7 @@ def tile_resourceallocationnetwork_pa_t_kernel(tc, g1, iab, sW2, sb2, sW3, sb3, 
             l2(s - 1)
             if s == 0:
                 x_t(2, [0, 1])
-                xt("w3", words_step2(w3raw[:]), [0], [3])
+                xt("w3", words_step2(w3raw[:]), [0], [2])
                 xe("w3", 0, False)
             rg(s, 0)
             x_e(s + LOOK, False)

from contextlib import ExitStack

import concourse.mybir as mybir
from concourse.masks import make_identity

F32 = mybir.dt.float32
BF16 = mybir.dt.bfloat16
U32 = mybir.dt.uint32
U8 = mybir.dt.uint8
FP8X4 = mybir.dt.float8_e4m3fn_x4
ACT = mybir.ActivationFunctionType
ALU = mybir.AluOpType
AX = mybir.AxisListType

P = 128
TOKENS = 6400
G = 512
G2 = 1024
NOUT = 128
SUBS = TOKENS // P
FLOPS = 2 * TOKENS * G * G2 + 2 * TOKENS * G2 * NOUT

LOOK = 2
LAG = 2


def tile_resourceallocationnetwork_pa_t_kernel(tc, g1, iab, sW2, sb2, sW3, sb3, out):
    nc = tc.nc
    nsubs = [2] + [4] * 11 + [2, 2]
    ns = len(nsubs)
    first = [sum(nsubs[:s]) for s in range(ns)]

    g1v = g1.flatten_outer_dims().rearrange("(p i) k -> p (i k)", i=SUBS)
    outv = out.flatten_outer_dims().rearrange("(p i) n -> p i n", i=SUBS)
    iabv = iab.rearrange("(p q) s -> p (q s)", p=P)
    w2v = sW2.rearrange("(g p t) k -> g p (t k)", g=2, t=4)
    b2v = sb2.rearrange("(g p t) -> p g t", g=2, t=4)

    with ExitStack() as ctx:
        const = ctx.enter_context(tc.tile_pool(name="const", bufs=1))
        raw = ctx.enter_context(tc.tile_pool(name="raw", bufs=1))
        keep = ctx.enter_context(tc.tile_pool(name="keep", bufs=1))
        xgp = ctx.enter_context(tc.tile_pool(name="xgp", bufs=5))
        hpp = ctx.enter_context(tc.tile_pool(name="hpp", bufs=6))
        hgp = ctx.enter_context(tc.tile_pool(name="hgp", bufs=3))
        hcp = ctx.enter_context(tc.tile_pool(name="hcp", bufs=6))
        epp = ctx.enter_context(tc.tile_pool(name="epp", bufs=4))
        otp = ctx.enter_context(tc.tile_pool(name="otp", bufs=6))
        sml = ctx.enter_context(tc.tile_pool(name="sml", bufs=6))
        psum = ctx.enter_context(tc.psum_pool(name="psum", bufs=1))

        ident = const.tile([P, P], F32, name="ident")
        make_identity(nc, ident[:])
        warm_in = const.tile([P, 1], F32, name="warm_in")
        warm_out = const.tile([P, 1], F32, name="warm_out")
        nc.vector.memset(warm_in[:], 0.0)
        nc.scalar.activation(out=warm_out[:], in_=warm_in[:], func=ACT.Exp)

        b2raw = const.tile([P, 2, 4], BF16, name="b2raw")
        c3raw = const.tile([P, NOUT], BF16, name="c3raw")
        iabraw = const.tile([P, SUBS], BF16, name="iabraw")
        nc.scalar.dma_start(out=b2raw[:], in_=b2v)

        w2raw = [raw.tile([P, 4 * G], BF16, name="w2raw%d" % g) for g in range(2)]
        w3raw = raw.tile([P, G2], BF16, name="w3raw")
        g1t = [raw.tile([P, nsubs[s] * G], BF16, name="g1t%d" % s) for s in range(ns)]

        def load_g1(s):
            nc.sync.dma_start(out=g1t[s][:], in_=g1v[:, G * first[s] : G * (first[s] + nsubs[s])])

        def load_w2(g, b):
            cols = slice(2 * G * b, 2 * G * b + 2 * G)
            nc.sync.dma_start(out=w2raw[g][:, cols], in_=w2v[g][:, cols])

        load_w2(0, 0)
        load_g1(0)
        load_w2(0, 1)
        load_w2(1, 0)
        load_w2(1, 1)
        load_g1(1)
        nc.sync.dma_start(out=w3raw[:], in_=sW3)
        for s in range(2, 5):
            load_g1(s)
        nc.sync.dma_start(out=c3raw[:], in_=sb3.partition_broadcast(P))
        nc.sync.dma_start(out=iabraw[:], in_=iabv)
        for s in range(5, ns):
            load_g1(s)

        w2c = [keep.tile([P, 512], U32, name="w2c%d" % g, align_bytes=64) for g in range(2)]
        w2s = [keep.tile([P, 512], U8, name="w2s%d" % g, align_bytes=64) for g in range(2)]
        w3c = keep.tile([P, 256], U32, name="w3c", align_bytes=64)
        w3s = keep.tile([P, 256], U8, name="w3s", align_bytes=64)
        xc = [keep.tile([P, P * nsubs[s]], U32, name="xc%d" % s, align_bytes=64) for s in range(ns)]
        xs = [keep.tile([P, P * nsubs[s]], U8, name="xs%d" % s, align_bytes=64) for s in range(ns)]
        b2f = const.tile([P, 8], F32, name="b2f")
        c3f = const.tile([P, NOUT], F32, name="c3f")
        iabf = const.tile([P, SUBS], F32, name="iabf")

        banks = {}
        grouped = {}

        def words_step2(tile_ap):
            w32 = tile_ap.bitcast(F32)
            return lambda j, u: w32[:, 256 * j + u : 256 * j + 256 : 2]

        def xt(key, words, blocks, bank_ids):
            for b in blocks:
                xp = psum.tile([P, 2, 256], F32, name="xp", tag="bank%d" % bank_ids[b - blocks[0]])
                for jj in range(2):
                    for u in range(2):
                        nc.tensor.transpose(xp[:, u, P * jj : P * jj + P], words(2 * b + jj, u), ident[:])
                banks[(key, b)] = xp

        def xe(key, b, on_scalar):
            if b == 0:
                grouped[key] = xgp.tile([P, 4 * P * 2], F32, name="xg", align_bytes=64)
            dst = grouped[key][:, 512 * b : 512 * b + 512].rearrange("p (w u) -> p w u", u=2)
            src = banks[(key, b)][:].rearrange("p u w -> p w u")
            if on_scalar:
                nc.scalar.copy(out=dst, in_=src)
            else:
                nc.vector.tensor_copy(out=dst, in_=src)

        def xq(key, nsub, codes, scales, b=0):
            nc.vector.quantize_mx(
                out=codes.bitcast(FP8X4),
                scales=scales,
                in_=grouped[key][:, 512 * b : 512 * b + 2 * P * nsub].bitcast(BF16),
            )

        def w2_t(g, b, bank):
            xt("w2%d" % g, words_step2(w2raw[g][:]), [b], [bank])

        def w2_q(g, b):
            cols = slice(256 * b, 256 * b + 256)
            xq("w2%d" % g, 2, w2c[g][:, cols], w2s[g][:, cols], b)

        def x_t(s, bank_ids):
            if 0 <= s < ns:
                xt(s, words_step2(g1t[s][:]), list(range(nsubs[s] // 2)), bank_ids)

        def x_e(s, second_on_scalar):
            if 0 <= s < ns:
                xe(s, 0, True)
                if nsubs[s] == 4:
                    xe(s, 1, second_on_scalar)

        def x_q(s):
            if 0 <= s < ns:
                xq(s, nsubs[s], xc[s][:], xs[s][:])

        hb = {}
        hp = {}
        hg = {}
        hc = {}
        hs = {}
        zb = {}
        nzc = {}
        mn = {}
        ex = {}
        ss = {}
        rs = {}

        def l1(s, g, t):
            if not 0 <= s < ns:
                return
            w = P * nsubs[s]
            hb_t = psum.tile([P, w], F32, name="hb", tag="bank%d" % (3 + ((2 * s + g) * 4 + t) % 5))
            nc.tensor.matmul_mx(
                out=hb_t[:],
                lhsT=w2c[g][:, P * t : P * t + P].bitcast(FP8X4),
                lhsT_scale=w2s[g][:, P * t : P * t + P],
                rhs=xc[s][:].bitcast(FP8X4),
                rhs_scale=xs[s][:],
                start=True,
                stop=True,
            )
            hb[(s, g, t)] = hb_t

        def ev(s, g, t):
            if not 0 <= s < ns:
                return
            w = P * nsubs[s]
            if t == 0:
                hp[(s, g)] = hpp.tile([P, 4, w], BF16, name="hp")
            nc.scalar.activation(
                out=hp[(s, g)][:, t, :],
                in_=hb[(s, g, t)][:],
                func=ACT.Relu,
                bias=b2f[:, 4 * g + t : 4 * g + t + 1],
                scale=1.0,
            )

        def rg(s, g):
            if not 0 <= s < ns:
                return
            w = P * nsubs[s]
            hg_t = hgp.tile([P, 4 * w], BF16, name="hg", align_bytes=64)
            nc.vector.tensor_copy(
                out=hg_t[:].rearrange("p (c i t) -> p c t i", i=4, t=4),
                in_=hp[(s, g)][:].rearrange("p t (c i) -> p c t i", i=4),
            )
            hg[(s, g)] = hg_t

        def hq(s, g):
            if not 0 <= s < ns:
                return
            w = P * nsubs[s]
            hc_t = hcp.tile([P, w], U32, name="hc", align_bytes=64)
            hs_t = hcp.tile([P, w], U8, name="hs", align_bytes=64)
            nc.vector.quantize_mx(out=hc_t[:].bitcast(FP8X4), scales=hs_t[:], in_=hg[(s, g)][:])
            hc[(s, g)] = hc_t
            hs[(s, g)] = hs_t

        def l2(s):
            if not 0 <= s < ns:
                return
            zb_t = psum.tile([P, 4, NOUT], F32, name="zb", tag="bank2")
            for j in range(nsubs[s]):
                for g in range(2):
                    nc.tensor.matmul_mx(
                        out=zb_t[:, j, :],
                        lhsT=hc[(s, g)][:, P * j : P * j + P].bitcast(FP8X4),
                        lhsT_scale=hs[(s, g)][:, P * j : P * j + P],
                        rhs=w3c[:, P * g : P * g + P].bitcast(FP8X4),
                        rhs_scale=w3s[:, P * g : P * g + P],
                        start=(g == 0),
                        stop=(g == 1),
                    )
            zb[s] = zb_t

        def stt(s):
            if not 0 <= s < ns:
                return
            n = nsubs[s]
            nzc_t = epp.tile([P, 4, NOUT], F32, name="nzc")
            nc.vector.scalar_tensor_tensor(
                out=nzc_t[:, :n, :],
                in0=zb[s][:, :n, :],
                scalar=-1.0,
                in1=c3f[:].unsqueeze(1).to_broadcast([P, n, NOUT]),
                op0=ALU.mult,
                op1=ALU.subtract,
            )
            nzc[s] = nzc_t

        def mnr(s):
            if not 0 <= s < ns:
                return
            n = nsubs[s]
            mn_t = sml.tile([P, 4], F32, name="mn")
            nc.vector.tensor_reduce(out=mn_t[:, :n], in_=nzc[s][:, :n, :], axis=AX.X, op=ALU.min)
            mn[s] = mn_t

        def ep2(s):
            if not 0 <= s < ns:
                return
            ex_t = epp.tile([P, 4, NOUT], F32, name="ex")
            ss_t = sml.tile([P, 4], F32, name="ss")
            for j in range(nsubs[s]):
                nc.scalar.activation(
                    out=ex_t[:, j, :],
                    in_=nzc[s][:, j, :],
                    func=ACT.Exp,
                    bias=mn[s][:, j : j + 1],
                    scale=-1.0,
                    accum_out=ss_t[:, j : j + 1],
                )
            ex[s] = ex_t
            ss[s] = ss_t

        def rc(s):
            if not 0 <= s < ns:
                return
            n = nsubs[s]
            rs_t = sml.tile([P, 4], F32, name="rs")
            nc.vector.reciprocal(out=rs_t[:, :n], in_=ss[s][:, :n])
            rs[s] = rs_t

        def ts(s):
            if not 0 <= s < ns:
                return
            n = nsubs[s]
            ot = otp.tile([P, 4, NOUT], F32, name="ot")
            for j in range(n):
                (nc.gpsimd if s < ns - 4 else nc.vector).tensor_scalar(
                    out=ot[:, j, :],
                    in0=ex[s][:, j, :],
                    scalar1=rs[s][:, j : j + 1],
                    scalar2=iabf[:, first[s] + j : first[s] + j + 1],
                    op0=ALU.mult,
                    op1=ALU.mult,
                )
            nc.sync.dma_start(out=outv[:, first[s] : first[s] + n, :], in_=ot[:, :n, :])

        w2_t(0, 0, 0)
        x_t(0, [1])
        w2_t(0, 1, 2)
        w2_t(1, 0, 7)
        xe("w20", 0, True)
        xe(0, 0, False)
        xe("w20", 1, True)
        w2_q(0, 0)
        x_q(0)
        w2_q(0, 1)
        nc.gpsimd.tensor_copy(out=b2f[:], in_=b2raw[:].rearrange("p g t -> p (g t)"))
        for t in range(4):
            l1(0, 0, t)
        xe("w21", 0, True)
        w2_t(1, 1, 0)
        xe("w21", 1, True)
        x_t(1, [1, 2])
        xe(1, 0, False)
        w2_q(1, 0)
        w2_q(1, 1)
        xe(1, 1, True)
        x_q(1)
        nc.gpsimd.tensor_copy(out=c3f[:], in_=c3raw[:])
        nc.gpsimd.tensor_copy(out=iabf[:], in_=iabraw[:])

        ctx.enter_context(tc.manual_schedule(engines={mybir.EngineType.PE}))
        for s in range(ns):
            if s > 0:
                x_q(s + 1)
            rg(s - 1, 1)
            rc(s - 4)
            stt(s - 2)
            hq(s - 1, 1)
            ts(s - 4)
            mnr(s - 2)
            ep2(s - 3)
            for t in range(4):
                ev(s, 0, t)
                l1(s, 1, t)
            l2(s - 1)
            if s == 0:
                x_t(2, [0, 1])
                xt("w3", words_step2(w3raw[:]), [0], [2])
                xe("w3", 0, False)
            rg(s, 0)
            x_e(s + LOOK, False)
            if s == 0:
                xq("w3", 2, w3c[:], w3s[:])
            hq(s, 0)
            for t in range(4):
                ev(s, 1, t)
                l1(s + 1, 0, t)
            x_t(s + LOOK + 1, [0, 1])

        ep2(ns - 3)
        stt(ns - 2)
        rc(ns - 4)
        rg(ns - 1, 1)
        mnr(ns - 2)
        hq(ns - 1, 1)
        l2(ns - 1)
        ts(ns - 4)
        rc(ns - 3)
        ep2(ns - 2)
        ts(ns - 3)
        stt(ns - 1)
        rc(ns - 2)
        mnr(ns - 1)
        ts(ns - 2)
        ep2(ns - 1)
        rc(ns - 1)
        ts(ns - 1)
